import numpy as np
import ml_dtypes


def mxq(x, axis, fmt="e4m3"):
    dtype, down = {"e4m3": (ml_dtypes.float8_e4m3fn, 7), "e5m2": (ml_dtypes.float8_e5m2, 14)}[fmt]
    v = np.moveaxis(np.asarray(x, np.float32).astype(ml_dtypes.bfloat16).astype(np.float64), axis, -1)
    blocks = v.reshape(v.shape[:-1] + (-1, 32))
    amax = np.abs(blocks).max(-1, keepdims=True)
    byte = np.maximum(np.where(amax > 0, np.frexp(amax)[1] - 1 + 127, 0) - down, 1)
    scale = np.exp2(byte - 127.0)
    codes = (blocks / scale).astype(np.float32).astype(dtype).astype(np.float64)
    return np.moveaxis((codes * scale).reshape(v.shape), -1, axis)


WIDE = False


def mx_kscale(k):
    if not WIDE:
        return np.ones(k)
    levels = np.array([10, -10, 5, -5, 0])
    a = np.random.permutation(np.resize(levels, k // 512 * 4)).reshape(k // 512, 4)
    idx = np.arange(k)
    return np.exp2(a[idx // 512, idx % 128 // 32])


BF16 = ml_dtypes.bfloat16


def bf(x):
    return np.asarray(x, np.float32).astype(BF16)


def f64(x):
    return np.asarray(x).astype(np.float64)


B, D_IN, UNITS = 1024, 512, 512


def sigmoid(v):
    return 1.0 / (1.0 + np.exp(-v))


def setup_inputs():
    s, t = mx_kscale(D_IN), mx_kscale(UNITS)
    sx, sh = 1.0 / np.sqrt(D_IN), 1.0 / np.sqrt(UNITS)
    return {"input_x": bf(np.random.standard_normal((B, D_IN)) * s),
            "input_h": bf(np.random.standard_normal((B, UNITS)) * t),
            "Wx_r": bf(np.random.standard_normal((D_IN, UNITS)) * sx / s[:, None]),
            "b_r": bf(np.random.standard_normal(UNITS) * 0.5),
            "Wh_r": bf(np.random.standard_normal((UNITS, UNITS)) * sh / t[:, None]),
            "Wx_h": bf(np.random.standard_normal((D_IN, UNITS)) * sx / s[:, None]),
            "b_h": bf(np.random.standard_normal(UNITS) * 0.5),
            "Wh_h": bf(np.random.standard_normal((UNITS, UNITS)) * sh / t[:, None])}


def reference(input_x, input_h, Wx_r, b_r, Wh_r, Wx_h, b_h, Wh_h):
    xq = mxq(f64(input_x), 1, "e4m3")
    hq = mxq(f64(input_h), 1, "e4m3")
    r = sigmoid((xq @ mxq(f64(Wx_r), 0, "e4m3")) + f64(b_r) + (hq @ mxq(f64(Wh_r), 0, "e4m3")))
    return np.tanh((xq @ mxq(f64(Wx_h), 0, "e4m3")) + f64(b_h) + r * (hq @ mxq(f64(Wh_h), 0, "e4m3")))

@@ -1,0 +1,218 @@
+from contextlib import ExitStack
+
+import concourse.mybir as mybir
+from concourse.masks import make_identity
+
+F32 = mybir.dt.float32
+BF16 = mybir.dt.bfloat16
+U32 = mybir.dt.uint32
+U8 = mybir.dt.uint8
+FP8X4 = mybir.dt.float8_e4m3fn_x4
+ACT = mybir.ActivationFunctionType
+ALU = mybir.AluOpType
+
+P = 128
+PACK = 4
+K = P * PACK
+BATCH = 1024
+UNITS = 512
+CHUNK = 512
+N_CHUNKS = BATCH // CHUNK
+ROW_TILES = CHUNK // P
+UNIT_TILES = UNITS // P
+WORDS = K // 2
+RUN = 4
+COLUMN_RUNS = UNITS // RUN
+VECTOR_RUNS = 5 * COLUMN_RUNS // 8
+
+FLOPS = 4 * 2 * BATCH * K * UNITS
+
+
+def tile_augru_pa_kernel(
+    tc, input_x, input_h, Wx_r, b_r, Wh_r, Wx_h, b_h, Wh_h, out
+):
+    nc = tc.nc
+    with ExitStack() as ctx:
+        const = ctx.enter_context(tc.tile_pool(name="const", bufs=1))
+        raw = ctx.enter_context(tc.tile_pool(name="raw", bufs=1))
+        mx = ctx.enter_context(tc.tile_pool(name="mx", bufs=1))
+        work = ctx.enter_context(tc.tile_pool(name="work", bufs=N_CHUNKS * UNIT_TILES))
+        banks = ctx.enter_context(tc.psum_pool(name="banks", bufs=8))
+        ctx.enter_context(tc.manual_schedule())
+
+        ident = const.tile([P, P], F32)
+        make_identity(nc, ident[:])
+        bias_rows = const.tile([P, P], BF16)
+        nc.vector.memset(bias_rows[:], 0.0)
+        nc.scalar.dma_start(out=bias_rows[0:UNIT_TILES, :], in_=b_r.rearrange("(i n) -> i n", n=P))
+        nc.scalar.dma_start(
+            out=bias_rows[UNIT_TILES : 2 * UNIT_TILES, :], in_=b_h.rearrange("(i n) -> i n", n=P)
+        )
+        warm = const.tile([P, 2], F32)
+        nc.vector.memset(warm[:], 0.0)
+        nc.scalar.activation(out=warm[:, 1:2], in_=warm[:, 0:1], func=ACT.Sigmoid)
+
+        def load_rows(name, rows):
+            tile = raw.tile([P, ROW_TILES * K], BF16, name=name)
+            nc.sync.dma_start(out=tile[:], in_=rows.rearrange("(p t) k -> p (t k)", t=ROW_TILES))
+            return tile
+
+        def load_weight(name, weight):
+            tile = raw.tile([P, PACK, UNITS], BF16, name=name)
+            nc.sync.dma_start(
+                out=tile[:].rearrange("q (u e) n -> q u e n", u=2),
+                in_=weight.rearrange("(u q e) n -> q u e n", u=2, e=2),
+            )
+            return tile
+
+        x_raw = [None] * N_CHUNKS
+        h_raw = [None] * N_CHUNKS
+        x_raw[0] = load_rows("x_raw0", input_x[0:CHUNK, :])
+        h_raw[0] = load_rows("h_raw0", input_h[0:CHUNK, :])
+        wxr_raw = load_weight("wxr_raw", Wx_r)
+        whr_raw = load_weight("whr_raw", Wh_r)
+        whh_raw = load_weight("whh_raw", Wh_h)
+        wxh_raw = load_weight("wxh_raw", Wx_h)
+        x_raw[1] = load_rows("x_raw1", input_x[CHUNK:BATCH, :])
+        h_raw[1] = load_rows("h_raw1", input_h[CHUNK:BATCH, :])
+
+        def transpose_rows(name, rows_raw):
+            grouped = mx.tile([P, CHUNK * PACK], BF16, name=name, align_bytes=64)
+            words = rows_raw[:].bitcast(F32)
+            grouped_words = grouped[:].bitcast(F32).rearrange("q (col u) -> q col u", u=2)
+            for half in range(2):
+                bank = banks.tile([P, CHUNK], F32, tag="bank")
+                planes = bank[:].rearrange("q (u col) -> q u col", u=2)
+                for local in range(2):
+                    first_word = (2 * half + local) * WORDS
+                    for u in range(2):
+                        nc.tensor.transpose(
+                            out=planes[:, u, local * P : (local + 1) * P],
+                            in_=words[:, first_word + u * P : first_word + (u + 1) * P],
+                            identity=ident[:],
+                        )
+                nc.scalar.copy(
+                    out=grouped_words[:, half * 2 * P : (half + 1) * 2 * P, :],
+                    in_=planes.rearrange("q u col -> q col u"),
+                )
+            return grouped[:]
+
+        def regroup_weight(name, weight_raw):
+            grouped = mx.tile([P, UNITS, PACK], BF16, name=name, align_bytes=64)
+            dst = grouped[:].rearrange("q (c i) t -> q c t i", i=RUN)
+            src = weight_raw[:].rearrange("q t (c i) -> q c t i", i=RUN)
+            nc.vector.tensor_copy(out=dst[:, :VECTOR_RUNS], in_=src[:, :VECTOR_RUNS])
+            nc.scalar.copy(out=dst[:, VECTOR_RUNS:], in_=src[:, VECTOR_RUNS:])
+            return grouped[:].rearrange("q n t -> q (n t)")
+
+        def quantise(name, grouped):
+            codes = mx.tile([P, CHUNK], U32, name=name + "_codes", align_bytes=64)
+            scales = mx.tile([P, CHUNK], U8, name=name + "_scales", align_bytes=64)
+            nc.vector.quantize_mx(out=codes[:].bitcast(FP8X4), scales=scales[:], in_=grouped)
+            return codes, scales
+
+        def mx_pass(acc, weight, i, rows, start, stop):
+            units = slice(i * P, (i + 1) * P)
+            nc.tensor.matmul_mx(
+                out=acc[:],
+                lhsT=weight[0][:, units].bitcast(FP8X4),
+                lhsT_scale=weight[1][:, units],
+                rhs=rows[0][:].bitcast(FP8X4),
+                rhs_scale=rows[1][:],
+                start=start,
+                stop=stop,
+            )
+
+        x_mx = [None] * N_CHUNKS
+        h_mx = [None] * N_CHUNKS
+        x_grouped = transpose_rows("x_grouped0", x_raw[0])
+        h_grouped = transpose_rows("h_grouped0", h_raw[0])
+        x_mx[0] = quantise("x0", x_grouped)
+        wxr_grouped = regroup_weight("wxr_grouped", wxr_raw)
+        h_mx[0] = quantise("h0", h_grouped)
+        whr_grouped = regroup_weight("whr_grouped", whr_raw)
+        wxr = quantise("wxr", wxr_grouped)
+
+        bias_square = const.tile([P, P], F32)
+        nc.vector.tensor_copy(out=bias_square[:], in_=bias_rows[:])
+        bias_bank = banks.tile([P, CHUNK], F32, tag="bank")
+        nc.tensor.transpose(out=bias_bank[:, 0:P], in_=bias_square[:], identity=ident[:])
+        bias = const.tile([P, 2 * UNIT_TILES], F32)
+        nc.vector.tensor_copy(out=bias[:], in_=bias_bank[:, 0 : 2 * UNIT_TILES])
+
+        whh_grouped = regroup_weight("whh_grouped", whh_raw)
+        whr = quantise("whr", whr_grouped)
+        wxh_grouped = regroup_weight("wxh_grouped", wxh_raw)
+        whh = quantise("whh", whh_grouped)
+        wxh = quantise("wxh", wxh_grouped)
+
+        gate = [[None] * UNIT_TILES for c in range(N_CHUNKS)]
+        gated = [[None] * UNIT_TILES for c in range(N_CHUNKS)]
+        summed = [[None] * UNIT_TILES for c in range(N_CHUNKS)]
+
+        def reset_gate(c, i):
+            acc = banks.tile([P, CHUNK], F32, tag="bank")
+            mx_pass(acc, wxr, i, x_mx[c], True, False)
+            mx_pass(acc, whr, i, h_mx[c], False, True)
+            r = work.tile([P, CHUNK], F32, tag="gate")
+            nc.scalar.activation(out=r[:], in_=acc[:], func=ACT.Sigmoid, bias=bias[:, i : i + 1])
+            gate[c][i] = r
+
+        def gated_state(c, i):
+            acc = banks.tile([P, CHUNK], F32, tag="bank")
+            mx_pass(acc, whh, i, h_mx[c], True, True)
+            product = work.tile([P, CHUNK], F32, tag="gated")
+            nc.vector.tensor_tensor(out=product[:], in0=gate[c][i][:], in1=acc[:], op=ALU.mult)
+            gated[c][i] = product
+
+        def candidate_sum(c, i):
+            acc = banks.tile([P, CHUNK], F32, tag="bank")
+            mx_pass(acc, wxh, i, x_mx[c], True, True)
+            total = work.tile([P, CHUNK], F32, tag="summed")
+            nc.vector.scalar_tensor_tensor(
+                out=total[:],
+                in0=acc[:],
+                scalar=bias[:, UNIT_TILES + i : UNIT_TILES + i + 1],
+                in1=gated[c][i][:],
+                op0=ALU.add,
+                op1=ALU.add,
+            )
+            summed[c][i] = total
+
+        def finish(c, i):
+            bank = banks.tile([P, CHUNK], F32, tag="bank")
+            for t in range(ROW_TILES):
+                nc.tensor.transpose(
+                    out=bank[:, t * P : (t + 1) * P],
+                    in_=summed[c][i][:, t * P : (t + 1) * P],
+                    identity=ident[:],
+                )
+            result = work.tile([P, CHUNK], F32, tag="result")
+            nc.scalar.activation(out=result[:], in_=bank[:], func=ACT.Tanh)
+            nc.sync.dma_start(
+                out=out[c * CHUNK : (c + 1) * CHUNK, i * P : (i + 1) * P].rearrange(
+                    "(p t) n -> p t n", t=ROW_TILES
+                ),
+                in_=result[:].rearrange("p (t n) -> p t n", t=ROW_TILES),
+            )
+
+        for i in range(UNIT_TILES):
+            reset_gate(0, i)
+        for i in range(UNIT_TILES):
+            gated_state(0, i)
+        x_grouped = transpose_rows("x_grouped1", x_raw[1])
+        h_grouped = transpose_rows("h_grouped1", h_raw[1])
+        x_mx[1] = quantise("x1", x_grouped)
+        h_mx[1] = quantise("h1", h_grouped)
+        for i in range(UNIT_TILES):
+            candidate_sum(0, i)
+        for i in range(UNIT_TILES):
+            reset_gate(1, i)
+        for i in range(UNIT_TILES):
+            gated_state(1, i)
+        for i in range(UNIT_TILES):
+            finish(0, i)
+        for i in range(UNIT_TILES):
+            candidate_sum(1, i)
+        for i in range(UNIT_TILES):
+            finish(1, i)

@@ -40,17 +40,19 @@ def tile_augru_pa_kernel(
         banks = ctx.enter_context(tc.psum_pool(name="banks", bufs=8))
         ctx.enter_context(tc.manual_schedule())
 
-        ident = const.tile([P, P], F32)
-        make_identity(nc, ident[:])
         bias_rows = const.tile([P, P], BF16)
-        nc.vector.memset(bias_rows[:], 0.0)
+        nc.gpsimd.memset(bias_rows[:], 0.0)
         nc.scalar.dma_start(out=bias_rows[0:UNIT_TILES, :], in_=b_r.rearrange("(i n) -> i n", n=P))
         nc.scalar.dma_start(
             out=bias_rows[UNIT_TILES : 2 * UNIT_TILES, :], in_=b_h.rearrange("(i n) -> i n", n=P)
         )
         warm = const.tile([P, 2], F32)
-        nc.vector.memset(warm[:], 0.0)
+        nc.gpsimd.memset(warm[:], 0.0)
         nc.scalar.activation(out=warm[:, 1:2], in_=warm[:, 0:1], func=ACT.Sigmoid)
+        ident = const.tile([P, P], F32)
+        make_identity(nc, ident[:])
+        bias_square = const.tile([P, P], F32)
+        nc.gpsimd.tensor_copy(out=bias_square[:], in_=bias_rows[:])
 
         def load_rows(name, rows):
             tile = raw.tile([P, ROW_TILES * K], BF16, name=name)
@@ -71,10 +73,10 @@ def tile_augru_pa_kernel(
         h_raw[0] = load_rows("h_raw0", input_h[0:CHUNK, :])
         wxr_raw = load_weight("wxr_raw", Wx_r)
         whr_raw = load_weight("whr_raw", Wh_r)
-        whh_raw = load_weight("whh_raw", Wh_h)
-        wxh_raw = load_weight("wxh_raw", Wx_h)
         x_raw[1] = load_rows("x_raw1", input_x[CHUNK:BATCH, :])
         h_raw[1] = load_rows("h_raw1", input_h[CHUNK:BATCH, :])
+        whh_raw = load_weight("whh_raw", Wh_h)
+        wxh_raw = load_weight("wxh_raw", Wx_h)
 
         def transpose_rows(name, rows_raw):
             grouped = mx.tile([P, CHUNK * PACK], BF16, name=name, align_bytes=64)
@@ -132,18 +134,18 @@ def tile_augru_pa_kernel(
         h_mx[0] = quantise("h0", h_grouped)
         whr_grouped = regroup_weight("whr_grouped", whr_raw)
         wxr = quantise("wxr", wxr_grouped)
-
-        bias_square = const.tile([P, P], F32)
-        nc.vector.tensor_copy(out=bias_square[:], in_=bias_rows[:])
+        whr = quantise("whr", whr_grouped)
+        x_grouped = transpose_rows("x_grouped1", x_raw[1])
+        whh_grouped = regroup_weight("whh_grouped", whh_raw)
+        x_mx[1] = quantise("x1", x_grouped)
+        whh = quantise("whh", whh_grouped)
+        h_grouped = transpose_rows("h_grouped1", h_raw[1])
+        wxh_grouped = regroup_weight("wxh_grouped", wxh_raw)
         bias_bank = banks.tile([P, CHUNK], F32, tag="bank")
         nc.tensor.transpose(out=bias_bank[:, 0:P], in_=bias_square[:], identity=ident[:])
         bias = const.tile([P, 2 * UNIT_TILES], F32)
         nc.vector.tensor_copy(out=bias[:], in_=bias_bank[:, 0 : 2 * UNIT_TILES])
-
-        whh_grouped = regroup_weight("whh_grouped", whh_raw)
-        whr = quantise("whr", whr_grouped)
-        wxh_grouped = regroup_weight("wxh_grouped", wxh_raw)
-        whh = quantise("whh", whh_grouped)
+        h_mx[1] = quantise("h1", h_grouped)
         wxh = quantise("wxh", wxh_grouped)
 
         gate = [[None] * UNIT_TILES for c in range(N_CHUNKS)]
@@ -200,10 +202,6 @@ def tile_augru_pa_kernel(
             reset_gate(0, i)
         for i in range(UNIT_TILES):
             gated_state(0, i)
-        x_grouped = transpose_rows("x_grouped1", x_raw[1])
-        h_grouped = transpose_rows("h_grouped1", h_raw[1])
-        x_mx[1] = quantise("x1", x_grouped)
-        h_mx[1] = quantise("h1", h_grouped)
         for i in range(UNIT_TILES):
             candidate_sum(0, i)
         for i in range(UNIT_TILES):

@@ -23,7 +23,7 @@ UNIT_TILES = UNITS // P
 WORDS = K // 2
 RUN = 4
 COLUMN_RUNS = UNITS // RUN
-VECTOR_RUNS = 5 * COLUMN_RUNS // 8
+VECTOR_RUNS = COLUMN_RUNS // 2
 
 FLOPS = 4 * 2 * BATCH * K * UNITS
 

@@ -23,7 +23,7 @@ UNIT_TILES = UNITS // P
 WORDS = K // 2
 RUN = 4
 COLUMN_RUNS = UNITS // RUN
-VECTOR_RUNS = COLUMN_RUNS // 2
+VECTOR_RUNS = 5 * COLUMN_RUNS // 8
 
 FLOPS = 4 * 2 * BATCH * K * UNITS
 
@@ -198,16 +198,17 @@ def tile_augru_pa_kernel(
                 in_=result[:].rearrange("p (t n) -> p t n", t=ROW_TILES),
             )
 
-        for i in range(UNIT_TILES):
-            reset_gate(0, i)
-        for i in range(UNIT_TILES):
-            gated_state(0, i)
+        def gate_and_state(c):
+            reset_gate(c, 0)
+            for i in range(1, UNIT_TILES):
+                reset_gate(c, i)
+                gated_state(c, i - 1)
+            gated_state(c, UNIT_TILES - 1)
+
+        gate_and_state(0)
         for i in range(UNIT_TILES):
             candidate_sum(0, i)
-        for i in range(UNIT_TILES):
-            reset_gate(1, i)
-        for i in range(UNIT_TILES):
-            gated_state(1, i)
+        gate_and_state(1)
         for i in range(UNIT_TILES):
             finish(0, i)
         for i in range(UNIT_TILES):

from contextlib import ExitStack

import concourse.mybir as mybir
from concourse.masks import make_identity

F32 = mybir.dt.float32
BF16 = mybir.dt.bfloat16
U32 = mybir.dt.uint32
U8 = mybir.dt.uint8
FP8X4 = mybir.dt.float8_e4m3fn_x4
ACT = mybir.ActivationFunctionType
ALU = mybir.AluOpType

P = 128
PACK = 4
K = P * PACK
BATCH = 1024
UNITS = 512
CHUNK = 512
N_CHUNKS = BATCH // CHUNK
ROW_TILES = CHUNK // P
UNIT_TILES = UNITS // P
WORDS = K // 2
RUN = 4
COLUMN_RUNS = UNITS // RUN
VECTOR_RUNS = 5 * COLUMN_RUNS // 8

FLOPS = 4 * 2 * BATCH * K * UNITS


def tile_augru_pa_kernel(
    tc, input_x, input_h, Wx_r, b_r, Wh_r, Wx_h, b_h, Wh_h, out
):
    nc = tc.nc
    with ExitStack() as ctx:
        const = ctx.enter_context(tc.tile_pool(name="const", bufs=1))
        raw = ctx.enter_context(tc.tile_pool(name="raw", bufs=1))
        mx = ctx.enter_context(tc.tile_pool(name="mx", bufs=1))
        work = ctx.enter_context(tc.tile_pool(name="work", bufs=N_CHUNKS * UNIT_TILES))
        banks = ctx.enter_context(tc.psum_pool(name="banks", bufs=8))
        ctx.enter_context(tc.manual_schedule())

        bias_rows = const.tile([P, P], BF16)
        nc.gpsimd.memset(bias_rows[:], 0.0)
        nc.scalar.dma_start(out=bias_rows[0:UNIT_TILES, :], in_=b_r.rearrange("(i n) -> i n", n=P))
        nc.scalar.dma_start(
            out=bias_rows[UNIT_TILES : 2 * UNIT_TILES, :], in_=b_h.rearrange("(i n) -> i n", n=P)
        )
        warm = const.tile([P, 2], F32)
        nc.gpsimd.memset(warm[:], 0.0)
        nc.scalar.activation(out=warm[:, 1:2], in_=warm[:, 0:1], func=ACT.Sigmoid)
        ident = const.tile([P, P], F32)
        make_identity(nc, ident[:])
        bias_square = const.tile([P, P], F32)
        nc.gpsimd.tensor_copy(out=bias_square[:], in_=bias_rows[:])

        def load_rows(name, rows):
            tile = raw.tile([P, ROW_TILES * K], BF16, name=name)
            nc.sync.dma_start(out=tile[:], in_=rows.rearrange("(p t) k -> p (t k)", t=ROW_TILES))
            return tile

        def load_weight(name, weight):
            tile = raw.tile([P, PACK, UNITS], BF16, name=name)
            nc.sync.dma_start(
                out=tile[:].rearrange("q (u e) n -> q u e n", u=2),
                in_=weight.rearrange("(u q e) n -> q u e n", u=2, e=2),
            )
            return tile

        x_raw = [None] * N_CHUNKS
        h_raw = [None] * N_CHUNKS
        x_raw[0] = load_rows("x_raw0", input_x[0:CHUNK, :])
        h_raw[0] = load_rows("h_raw0", input_h[0:CHUNK, :])
        wxr_raw = load_weight("wxr_raw", Wx_r)
        whr_raw = load_weight("whr_raw", Wh_r)
        x_raw[1] = load_rows("x_raw1", input_x[CHUNK:BATCH, :])
        h_raw[1] = load_rows("h_raw1", input_h[CHUNK:BATCH, :])
        whh_raw = load_weight("whh_raw", Wh_h)
        wxh_raw = load_weight("wxh_raw", Wx_h)

        def transpose_rows(name, rows_raw):
            grouped = mx.tile([P, CHUNK * PACK], BF16, name=name, align_bytes=64)
            words = rows_raw[:].bitcast(F32)
            grouped_words = grouped[:].bitcast(F32).rearrange("q (col u) -> q col u", u=2)
            for half in range(2):
                bank = banks.tile([P, CHUNK], F32, tag="bank")
                planes = bank[:].rearrange("q (u col) -> q u col", u=2)
                for local in range(2):
                    first_word = (2 * half + local) * WORDS
                    for u in range(2):
                        nc.tensor.transpose(
                            out=planes[:, u, local * P : (local + 1) * P],
                            in_=words[:, first_word + u * P : first_word + (u + 1) * P],
                            identity=ident[:],
                        )
                nc.scalar.copy(
                    out=grouped_words[:, half * 2 * P : (half + 1) * 2 * P, :],
                    in_=planes.rearrange("q u col -> q col u"),
                )
            return grouped[:]

        def regroup_weight(name, weight_raw):
            grouped = mx.tile([P, UNITS, PACK], BF16, name=name, align_bytes=64)
            dst = grouped[:].rearrange("q (c i) t -> q c t i", i=RUN)
            src = weight_raw[:].rearrange("q t (c i) -> q c t i", i=RUN)
            nc.vector.tensor_copy(out=dst[:, :VECTOR_RUNS], in_=src[:, :VECTOR_RUNS])
            nc.scalar.copy(out=dst[:, VECTOR_RUNS:], in_=src[:, VECTOR_RUNS:])
            return grouped[:].rearrange("q n t -> q (n t)")

        def quantise(name, grouped):
            codes = mx.tile([P, CHUNK], U32, name=name + "_codes", align_bytes=64)
            scales = mx.tile([P, CHUNK], U8, name=name + "_scales", align_bytes=64)
            nc.vector.quantize_mx(out=codes[:].bitcast(FP8X4), scales=scales[:], in_=grouped)
            return codes, scales

        def mx_pass(acc, weight, i, rows, start, stop):
            units = slice(i * P, (i + 1) * P)
            nc.tensor.matmul_mx(
                out=acc[:],
                lhsT=weight[0][:, units].bitcast(FP8X4),
                lhsT_scale=weight[1][:, units],
                rhs=rows[0][:].bitcast(FP8X4),
                rhs_scale=rows[1][:],
                start=start,
                stop=stop,
            )

        x_mx = [None] * N_CHUNKS
        h_mx = [None] * N_CHUNKS
        x_grouped = transpose_rows("x_grouped0", x_raw[0])
        h_grouped = transpose_rows("h_grouped0", h_raw[0])
        x_mx[0] = quantise("x0", x_grouped)
        wxr_grouped = regroup_weight("wxr_grouped", wxr_raw)
        h_mx[0] = quantise("h0", h_grouped)
        whr_grouped = regroup_weight("whr_grouped", whr_raw)
        wxr = quantise("wxr", wxr_grouped)
        whr = quantise("whr", whr_grouped)
        x_grouped = transpose_rows("x_grouped1", x_raw[1])
        whh_grouped = regroup_weight("whh_grouped", whh_raw)
        x_mx[1] = quantise("x1", x_grouped)
        whh = quantise("whh", whh_grouped)
        h_grouped = transpose_rows("h_grouped1", h_raw[1])
        wxh_grouped = regroup_weight("wxh_grouped", wxh_raw)
        bias_bank = banks.tile([P, CHUNK], F32, tag="bank")
        nc.tensor.transpose(out=bias_bank[:, 0:P], in_=bias_square[:], identity=ident[:])
        bias = const.tile([P, 2 * UNIT_TILES], F32)
        nc.vector.tensor_copy(out=bias[:], in_=bias_bank[:, 0 : 2 * UNIT_TILES])
        h_mx[1] = quantise("h1", h_grouped)
        wxh = quantise("wxh", wxh_grouped)

        gate = [[None] * UNIT_TILES for c in range(N_CHUNKS)]
        gated = [[None] * UNIT_TILES for c in range(N_CHUNKS)]
        summed = [[None] * UNIT_TILES for c in range(N_CHUNKS)]

        def reset_gate(c, i):
            acc = banks.tile([P, CHUNK], F32, tag="bank")
            mx_pass(acc, wxr, i, x_mx[c], True, False)
            mx_pass(acc, whr, i, h_mx[c], False, True)
            r = work.tile([P, CHUNK], F32, tag="gate")
            nc.scalar.activation(out=r[:], in_=acc[:], func=ACT.Sigmoid, bias=bias[:, i : i + 1])
            gate[c][i] = r

        def gated_state(c, i):
            acc = banks.tile([P, CHUNK], F32, tag="bank")
            mx_pass(acc, whh, i, h_mx[c], True, True)
            product = work.tile([P, CHUNK], F32, tag="gated")
            nc.vector.tensor_tensor(out=product[:], in0=gate[c][i][:], in1=acc[:], op=ALU.mult)
            gated[c][i] = product

        def candidate_sum(c, i):
            acc = banks.tile([P, CHUNK], F32, tag="bank")
            mx_pass(acc, wxh, i, x_mx[c], True, True)
            total = work.tile([P, CHUNK], F32, tag="summed")
            nc.vector.scalar_tensor_tensor(
                out=total[:],
                in0=acc[:],
                scalar=bias[:, UNIT_TILES + i : UNIT_TILES + i + 1],
                in1=gated[c][i][:],
                op0=ALU.add,
                op1=ALU.add,
            )
            summed[c][i] = total

        def finish(c, i):
            bank = banks.tile([P, CHUNK], F32, tag="bank")
            for t in range(ROW_TILES):
                nc.tensor.transpose(
                    out=bank[:, t * P : (t + 1) * P],
                    in_=summed[c][i][:, t * P : (t + 1) * P],
                    identity=ident[:],
                )
            result = work.tile([P, CHUNK], F32, tag="result")
            nc.scalar.activation(out=result[:], in_=bank[:], func=ACT.Tanh)
            nc.sync.dma_start(
                out=out[c * CHUNK : (c + 1) * CHUNK, i * P : (i + 1) * P].rearrange(
                    "(p t) n -> p t n", t=ROW_TILES
                ),
                in_=result[:].rearrange("p (t n) -> p t n", t=ROW_TILES),
            )

        def gate_and_state(c):
            reset_gate(c, 0)
            for i in range(1, UNIT_TILES):
                reset_gate(c, i)
                gated_state(c, i - 1)
            gated_state(c, UNIT_TILES - 1)

        gate_and_state(0)
        for i in range(UNIT_TILES):
            candidate_sum(0, i)
        gate_and_state(1)
        for i in range(UNIT_TILES):
            finish(0, i)
        for i in range(UNIT_TILES):
            candidate_sum(1, i)
        for i in range(UNIT_TILES):
            finish(1, i)
